import numpy as np
import ml_dtypes


def mxq(x, axis, fmt="e4m3"):
    dtype, down = {"e4m3": (ml_dtypes.float8_e4m3fn, 7), "e5m2": (ml_dtypes.float8_e5m2, 14)}[fmt]
    v = np.moveaxis(np.asarray(x, np.float32).astype(ml_dtypes.bfloat16).astype(np.float64), axis, -1)
    blocks = v.reshape(v.shape[:-1] + (-1, 32))
    amax = np.abs(blocks).max(-1, keepdims=True)
    byte = np.maximum(np.where(amax > 0, np.frexp(amax)[1] - 1 + 127, 0) - down, 1)
    scale = np.exp2(byte - 127.0)
    codes = (blocks / scale).astype(np.float32).astype(dtype).astype(np.float64)
    return np.moveaxis((codes * scale).reshape(v.shape), -1, axis)


WIDE = False


def mx_kscale(k):
    if not WIDE:
        return np.ones(k)
    levels = np.array([10, -10, 5, -5, 0])
    a = np.random.permutation(np.resize(levels, k // 512 * 4)).reshape(k // 512, 4)
    idx = np.arange(k)
    return np.exp2(a[idx // 512, idx % 128 // 32])


BF16 = ml_dtypes.bfloat16


def bf(x):
    return np.asarray(x, np.float32).astype(BF16)


def f64(x):
    return np.asarray(x).astype(np.float64)


L, R, T, H, F = 4, 4, 128, 512, 512


def setup_inputs():
    s, t = mx_kscale(H), mx_kscale(F)
    return {"x": bf(np.random.standard_normal((R, T, H)) * s),
            "w_first": bf(np.random.standard_normal((R, H, F)) / np.sqrt(R * H) / s[:, None] * t),
            "w_second": bf(np.random.standard_normal((R, F, H)) / np.sqrt(R * F) / t[:, None])}


def reference(x, w_first, w_second):
    y = mxq(f64(x), 2, "e4m3") @ mxq(f64(w_first), 1, "e4m3")
    reduced = y.sum(0)
    z = mxq(reduced, 1, "e4m3")[None] @ mxq(f64(w_second), 1, "e4m3")
    total = z.sum(0)
    return np.broadcast_to(total[None], z.shape).copy()

@@ -1,0 +1,150 @@
+from contextlib import ExitStack
+
+import concourse.mybir as mybir
+from concourse.masks import make_identity
+
+BF16 = mybir.dt.bfloat16
+F32 = mybir.dt.float32
+U32 = mybir.dt.uint32
+U8 = mybir.dt.uint8
+FP8X4 = mybir.dt.float8_e4m3fn_x4
+
+P = 128
+PACK = 4
+RANKS = 4
+TOKENS = 128
+WIDTH = 512
+HALF = WIDTH // 2
+BANK_RANKS = 2
+
+FLOPS = 2 * 2 * RANKS * TOKENS * WIDTH * WIDTH
+
+
+def regroup(nc, raw, grouped):
+    for engine_copy, cols in (
+        (nc.vector.tensor_copy, slice(0, HALF)),
+        (nc.scalar.copy, slice(HALF, WIDTH)),
+    ):
+        engine_copy(
+            out=grouped[:, cols, :].rearrange("p (c i) t -> p c t i", i=4),
+            in_=raw[:, :, cols].rearrange("p t (c i) -> p c t i", i=4),
+        )
+
+
+def quantise(nc, grouped, codes, scales):
+    nc.vector.quantize_mx(
+        out=codes[:].bitcast(FP8X4),
+        scales=scales[:],
+        in_=grouped[:].rearrange("p c t -> p (c t)"),
+    )
+
+
+def tile_multilayerallreduce_pa_s_kernel(tc, x, w_first, w_second, out):
+    nc = tc.nc
+    with ExitStack() as ctx:
+        keep = ctx.enter_context(tc.tile_pool(name="keep", bufs=1))
+        psum = ctx.enter_context(tc.psum_pool(name="psum", bufs=1))
+        ctx.enter_context(tc.manual_schedule())
+
+        x_rows = keep.tile([TOKENS, RANKS, WIDTH], BF16)
+        nc.sync.dma_start(out=x_rows[:], in_=x.rearrange("r t k -> t r k"))
+        shards = []
+        for r in range(RANKS):
+            raw = keep.tile([P, PACK, WIDTH], BF16, name="raw_first%d" % r)
+            nc.sync.dma_start(
+                out=raw[:].rearrange("p (u e) c -> p u (e c)", u=2),
+                in_=w_first[r].rearrange("(u p e) c -> p u (e c)", u=2, e=2),
+            )
+            shards.append(raw)
+        for r in range(RANKS):
+            raw = keep.tile([P, PACK, WIDTH], BF16, name="raw_second%d" % r)
+            nc.sync.dma_start(out=raw[:], in_=w_second[r].rearrange("(t p) c -> p t c", p=P))
+            shards.append(raw)
+        grouped = [
+            keep.tile([P, WIDTH, PACK], BF16, align_bytes=64, name="grouped%d" % s)
+            for s in range(2 * RANKS)
+        ]
+        codes = [
+            keep.tile([P, WIDTH], U32, align_bytes=64, name="codes%d" % s)
+            for s in range(2 * RANKS)
+        ]
+        scales = [
+            keep.tile([P, WIDTH], U8, align_bytes=64, name="scales%d" % s)
+            for s in range(2 * RANKS)
+        ]
+
+        identity = keep.tile([P, P], F32)
+        make_identity(nc, identity[:])
+        x_words = x_rows[:].rearrange("t r k -> t (r k)").bitcast(F32)
+        x_grouped = keep.tile([P, RANKS * TOKENS, PACK], BF16, align_bytes=64)
+        x_grouped_words = (
+            x_grouped[:]
+            .rearrange("p c t -> p (c t)")
+            .bitcast(F32)
+            .rearrange("p (r c u) -> p r c u", r=RANKS, u=2)
+        )
+        for b, engine_copy in enumerate((nc.vector.tensor_copy, nc.scalar.copy)):
+            x_bank = psum.tile([P, BANK_RANKS, 2, TOKENS], F32, name="x_bank%d" % b)
+            for i in range(BANK_RANKS):
+                for u in range(2):
+                    first_word = ((b * BANK_RANKS + i) * 2 + u) * P
+                    nc.tensor.transpose(
+                        x_bank[:, i, u, :], x_words[:, first_word : first_word + P], identity[:]
+                    )
+            engine_copy(
+                out=x_grouped_words[:, b * BANK_RANKS : (b + 1) * BANK_RANKS],
+                in_=x_bank[:].rearrange("p r u c -> p r c u"),
+            )
+        x_codes = keep.tile([P, RANKS * TOKENS], U32, align_bytes=64)
+        x_scales = keep.tile([P, RANKS * TOKENS], U8, align_bytes=64)
+
+        regroup(nc, shards[0], grouped[0])
+        quantise(nc, x_grouped, x_codes, x_scales)
+        for s in range(1, RANKS + 1):
+            regroup(nc, shards[s], grouped[s])
+            quantise(nc, grouped[s - 1], codes[s - 1], scales[s - 1])
+
+        hidden_sums = psum.tile([P, PACK, TOKENS], F32)
+        for t in range(PACK):
+            for r in range(RANKS):
+                nc.tensor.matmul_mx(
+                    out=hidden_sums[:, t, :],
+                    lhsT=codes[r][:, t * P : (t + 1) * P].bitcast(FP8X4),
+                    lhsT_scale=scales[r][:, t * P : (t + 1) * P],
+                    rhs=x_codes[:, r * TOKENS : (r + 1) * TOKENS].bitcast(FP8X4),
+                    rhs_scale=x_scales[:, r * TOKENS : (r + 1) * TOKENS],
+                    start=(r == 0),
+                    stop=(r == RANKS - 1),
+                )
+
+        for s in range(RANKS + 1, 2 * RANKS - 1):
+            regroup(nc, shards[s], grouped[s])
+            quantise(nc, grouped[s - 1], codes[s - 1], scales[s - 1])
+
+        hidden_grouped = keep.tile([P, TOKENS, PACK], BF16, align_bytes=64)
+        hidden_codes = keep.tile([P, TOKENS], U32, align_bytes=64)
+        hidden_scales = keep.tile([P, TOKENS], U8, align_bytes=64)
+        nc.scalar.copy(out=hidden_grouped[:], in_=hidden_sums[:].rearrange("p t c -> p c t"))
+        last = 2 * RANKS - 1
+        regroup(nc, shards[last], grouped[last])
+        quantise(nc, hidden_grouped, hidden_codes, hidden_scales)
+        quantise(nc, grouped[last - 1], codes[last - 1], scales[last - 1])
+        quantise(nc, grouped[last], codes[last], scales[last])
+
+        total_sums = [psum.tile([TOKENS, HALF], F32, name="total_sums%d" % h) for h in range(2)]
+        for r in range(RANKS):
+            for h in range(2):
+                nc.tensor.matmul_mx(
+                    out=total_sums[h][:],
+                    lhsT=hidden_codes[:].bitcast(FP8X4),
+                    lhsT_scale=hidden_scales[:],
+                    rhs=codes[RANKS + r][:, h * HALF : (h + 1) * HALF].bitcast(FP8X4),
+                    rhs_scale=scales[RANKS + r][:, h * HALF : (h + 1) * HALF],
+                    start=(r == 0),
+                    stop=(r == RANKS - 1),
+                )
+        total = keep.tile([TOKENS, WIDTH], F32)
+        nc.vector.tensor_copy(out=total[:, 0:HALF], in_=total_sums[0][:])
+        nc.scalar.copy(out=total[:, HALF:WIDTH], in_=total_sums[1][:])
+        for r in range(RANKS):
+            nc.sync.dma_start(out=out[r], in_=total[:])

@@ -11,6 +11,7 @@ FP8X4 = mybir.dt.float8_e4m3fn_x4
 
 P = 128
 PACK = 4
+RUN = 4
 RANKS = 4
 TOKENS = 128
 WIDTH = 512
@@ -20,23 +21,14 @@ BANK_RANKS = 2
 FLOPS = 2 * 2 * RANKS * TOKENS * WIDTH * WIDTH
 
 
-def regroup(nc, raw, grouped):
-    for engine_copy, cols in (
-        (nc.vector.tensor_copy, slice(0, HALF)),
-        (nc.scalar.copy, slice(HALF, WIDTH)),
-    ):
-        engine_copy(
-            out=grouped[:, cols, :].rearrange("p (c i) t -> p c t i", i=4),
-            in_=raw[:, :, cols].rearrange("p t (c i) -> p c t i", i=4),
-        )
+def regroup(nc, raw_runs, grouped_runs):
+    middle = raw_runs.shape[1] // 2
+    nc.vector.tensor_copy(out=grouped_runs[:, :middle], in_=raw_runs[:, :middle])
+    nc.scalar.copy(out=grouped_runs[:, middle:], in_=raw_runs[:, middle:])
 
 
 def quantise(nc, grouped, codes, scales):
-    nc.vector.quantize_mx(
-        out=codes[:].bitcast(FP8X4),
-        scales=scales[:],
-        in_=grouped[:].rearrange("p c t -> p (c t)"),
-    )
+    nc.vector.quantize_mx(out=codes.bitcast(FP8X4), scales=scales, in_=grouped)
 
 
 def tile_multilayerallreduce_pa_s_kernel(tc, x, w_first, w_second, out):
@@ -47,21 +39,19 @@ def tile_multilayerallreduce_pa_s_kernel(tc, x, w_first, w_second, out):
         ctx.enter_context(tc.manual_schedule())
 
         x_rows = keep.tile([TOKENS, RANKS, WIDTH], BF16)
-        nc.sync.dma_start(out=x_rows[:], in_=x.rearrange("r t k -> t r k"))
-        shards = []
-        for r in range(RANKS):
-            raw = keep.tile([P, PACK, WIDTH], BF16, name="raw_first%d" % r)
-            nc.sync.dma_start(
-                out=raw[:].rearrange("p (u e) c -> p u (e c)", u=2),
-                in_=w_first[r].rearrange("(u p e) c -> p u (e c)", u=2, e=2),
-            )
-            shards.append(raw)
-        for r in range(RANKS):
-            raw = keep.tile([P, PACK, WIDTH], BF16, name="raw_second%d" % r)
-            nc.sync.dma_start(out=raw[:], in_=w_second[r].rearrange("(t p) c -> p t c", p=P))
-            shards.append(raw)
+        for b in range(RANKS // BANK_RANKS):
+            ranks = slice(b * BANK_RANKS, (b + 1) * BANK_RANKS)
+            nc.sync.dma_start(out=x_rows[:, ranks, :], in_=x[ranks].rearrange("r t k -> t r k"))
+        raw = []
+        for weights in (w_first, w_second):
+            for r in range(RANKS):
+                shard = keep.tile([P, PACK, WIDTH], BF16, name="raw%d" % len(raw))
+                nc.sync.dma_start(
+                    out=shard[:], in_=weights[r].rearrange("(p t) c -> p t c", t=PACK)
+                )
+                raw.append(shard[:].rearrange("p t (c i) -> p c t i", i=RUN))
         grouped = [
-            keep.tile([P, WIDTH, PACK], BF16, align_bytes=64, name="grouped%d" % s)
+            keep.tile([P, WIDTH * PACK], BF16, align_bytes=64, name="grouped%d" % s)
             for s in range(2 * RANKS)
         ]
         codes = [
@@ -75,21 +65,20 @@ def tile_multilayerallreduce_pa_s_kernel(tc, x, w_first, w_second, out):
 
         identity = keep.tile([P, P], F32)
         make_identity(nc, identity[:])
-        x_words = x_rows[:].rearrange("t r k -> t (r k)").bitcast(F32)
-        x_grouped = keep.tile([P, RANKS * TOKENS, PACK], BF16, align_bytes=64)
-        x_grouped_words = (
-            x_grouped[:]
-            .rearrange("p c t -> p (c t)")
+        x_words = (
+            x_rows[:]
+            .rearrange("t r k -> t (r k)")
             .bitcast(F32)
-            .rearrange("p (r c u) -> p r c u", r=RANKS, u=2)
+            .rearrange("t (r p u) -> t r u p", r=RANKS, u=2)
         )
+        x_grouped = keep.tile([P, RANKS * TOKENS * PACK], BF16, align_bytes=64)
+        x_grouped_words = x_grouped[:].bitcast(F32).rearrange("p (r c u) -> p r c u", r=RANKS, u=2)
         for b, engine_copy in enumerate((nc.vector.tensor_copy, nc.scalar.copy)):
             x_bank = psum.tile([P, BANK_RANKS, 2, TOKENS], F32, name="x_bank%d" % b)
             for i in range(BANK_RANKS):
                 for u in range(2):
-                    first_word = ((b * BANK_RANKS + i) * 2 + u) * P
                     nc.tensor.transpose(
-                        x_bank[:, i, u, :], x_words[:, first_word : first_word + P], identity[:]
+                        x_bank[:, i, u, :], x_words[:, b * BANK_RANKS + i, u, :], identity[:]
                     )
             engine_copy(
                 out=x_grouped_words[:, b * BANK_RANKS : (b + 1) * BANK_RANKS],
@@ -98,53 +87,75 @@ def tile_multilayerallreduce_pa_s_kernel(tc, x, w_first, w_second, out):
         x_codes = keep.tile([P, RANKS * TOKENS], U32, align_bytes=64)
         x_scales = keep.tile([P, RANKS * TOKENS], U8, align_bytes=64)
 
-        regroup(nc, shards[0], grouped[0])
-        quantise(nc, x_grouped, x_codes, x_scales)
-        for s in range(1, RANKS + 1):
-            regroup(nc, shards[s], grouped[s])
-            quantise(nc, grouped[s - 1], codes[s - 1], scales[s - 1])
+        for s in range(RANKS):
+            regroup(nc, raw[s], grouped[s][:].rearrange("p (i c t) -> p c t i", i=RUN, t=PACK))
+            if s == 0:
+                quantise(nc, x_grouped[:], x_codes[:], x_scales[:])
+            else:
+                quantise(nc, grouped[s - 1][:], codes[s - 1][:], scales[s - 1][:])
+        quantise(nc, grouped[RANKS - 1][:], codes[RANKS - 1][:], scales[RANKS - 1][:])
 
         hidden_sums = psum.tile([P, PACK, TOKENS], F32)
-        for t in range(PACK):
+        for i in range(PACK):
             for r in range(RANKS):
                 nc.tensor.matmul_mx(
-                    out=hidden_sums[:, t, :],
-                    lhsT=codes[r][:, t * P : (t + 1) * P].bitcast(FP8X4),
-                    lhsT_scale=scales[r][:, t * P : (t + 1) * P],
+                    out=hidden_sums[:, i, :],
+                    lhsT=codes[r][:, i * P : (i + 1) * P].bitcast(FP8X4),
+                    lhsT_scale=scales[r][:, i * P : (i + 1) * P],
                     rhs=x_codes[:, r * TOKENS : (r + 1) * TOKENS].bitcast(FP8X4),
                     rhs_scale=x_scales[:, r * TOKENS : (r + 1) * TOKENS],
                     start=(r == 0),
                     stop=(r == RANKS - 1),
                 )
 
-        for s in range(RANKS + 1, 2 * RANKS - 1):
-            regroup(nc, shards[s], grouped[s])
-            quantise(nc, grouped[s - 1], codes[s - 1], scales[s - 1])
+        second = [
+            grouped[RANKS + r][:].rearrange("p (c i t) -> p c t i", i=RUN, t=PACK)
+            for r in range(RANKS)
+        ]
+        last = RANKS - 1
+        for r in range(last):
+            regroup(nc, raw[RANKS + r], second[r])
+            if r > 0:
+                quantise(nc, grouped[RANKS + r - 1][:], codes[RANKS + r - 1][:], scales[RANKS + r - 1][:])
 
         hidden_grouped = keep.tile([P, TOKENS, PACK], BF16, align_bytes=64)
         hidden_codes = keep.tile([P, TOKENS], U32, align_bytes=64)
         hidden_scales = keep.tile([P, TOKENS], U8, align_bytes=64)
-        nc.scalar.copy(out=hidden_grouped[:], in_=hidden_sums[:].rearrange("p t c -> p c t"))
-        last = 2 * RANKS - 1
-        regroup(nc, shards[last], grouped[last])
-        quantise(nc, hidden_grouped, hidden_codes, hidden_scales)
-        quantise(nc, grouped[last - 1], codes[last - 1], scales[last - 1])
-        quantise(nc, grouped[last], codes[last], scales[last])
+        nc.scalar.copy(out=hidden_grouped[:], in_=hidden_sums[:].rearrange("p i c -> p c i"))
+        quantise(nc, grouped[RANKS + last - 1][:], codes[RANKS + last - 1][:], scales[RANKS + last - 1][:])
+        quantise(nc, hidden_grouped[:].rearrange("p c i -> p (c i)"), hidden_codes[:], hidden_scales[:])
 
         total_sums = [psum.tile([TOKENS, HALF], F32, name="total_sums%d" % h) for h in range(2)]
-        for r in range(RANKS):
+
+        def second_layer_pass(r, h):
+            cols = slice(h * HALF, (h + 1) * HALF)
+            nc.tensor.matmul_mx(
+                out=total_sums[h][:],
+                lhsT=hidden_codes[:].bitcast(FP8X4),
+                lhsT_scale=hidden_scales[:],
+                rhs=codes[RANKS + r][:, cols].bitcast(FP8X4),
+                rhs_scale=scales[RANKS + r][:, cols],
+                start=(r == 0),
+                stop=(r == last),
+            )
+
+        for r in range(last):
             for h in range(2):
-                nc.tensor.matmul_mx(
-                    out=total_sums[h][:],
-                    lhsT=hidden_codes[:].bitcast(FP8X4),
-                    lhsT_scale=hidden_scales[:],
-                    rhs=codes[RANKS + r][:, h * HALF : (h + 1) * HALF].bitcast(FP8X4),
-                    rhs_scale=scales[RANKS + r][:, h * HALF : (h + 1) * HALF],
-                    start=(r == 0),
-                    stop=(r == RANKS - 1),
-                )
-        total = keep.tile([TOKENS, WIDTH], F32)
-        nc.vector.tensor_copy(out=total[:, 0:HALF], in_=total_sums[0][:])
-        nc.scalar.copy(out=total[:, HALF:WIDTH], in_=total_sums[1][:])
-        for r in range(RANKS):
-            nc.sync.dma_start(out=out[r], in_=total[:])
+                second_layer_pass(r, h)
+
+        half_runs = HALF // RUN
+        for h in range(2):
+            runs = slice(h * half_runs, (h + 1) * half_runs)
+            regroup(nc, raw[RANKS + last][:, runs], second[last][:, runs])
+        for h, engine_copy in enumerate((nc.scalar.copy, nc.vector.tensor_copy)):
+            quantise(
+                nc,
+                grouped[RANKS + last][:, h * HALF * PACK : (h + 1) * HALF * PACK],
+                codes[RANKS + last][:, h * HALF : (h + 1) * HALF],
+                scales[RANKS + last][:, h * HALF : (h + 1) * HALF],
+            )
+            second_layer_pass(last, h)
+            total = keep.tile([TOKENS, HALF], F32, name="total%d" % h)
+            engine_copy(out=total[:], in_=total_sums[h][:])
+            for r in range(RANKS):
+                nc.sync.dma_start(out=out[r, :, h * HALF : (h + 1) * HALF], in_=total[:])

@@ -13,22 +13,12 @@ P = 128
 PACK = 4
 RUN = 4
 RANKS = 4
+SHARDS = 2 * RANKS
 TOKENS = 128
 WIDTH = 512
 HALF = WIDTH // 2
-BANK_RANKS = 2
 
 FLOPS = 2 * 2 * RANKS * TOKENS * WIDTH * WIDTH
-
-
-def regroup(nc, raw_runs, grouped_runs):
-    middle = raw_runs.shape[1] // 2
-    nc.vector.tensor_copy(out=grouped_runs[:, :middle], in_=raw_runs[:, :middle])
-    nc.scalar.copy(out=grouped_runs[:, middle:], in_=raw_runs[:, middle:])
-
-
-def quantise(nc, grouped, codes, scales):
-    nc.vector.quantize_mx(out=codes.bitcast(FP8X4), scales=scales, in_=grouped)
 
 
 def tile_multilayerallreduce_pa_s_kernel(tc, x, w_first, w_second, out):
@@ -39,29 +29,46 @@ def tile_multilayerallreduce_pa_s_kernel(tc, x, w_first, w_second, out):
         ctx.enter_context(tc.manual_schedule())
 
         x_rows = keep.tile([TOKENS, RANKS, WIDTH], BF16)
-        for b in range(RANKS // BANK_RANKS):
-            ranks = slice(b * BANK_RANKS, (b + 1) * BANK_RANKS)
-            nc.sync.dma_start(out=x_rows[:, ranks, :], in_=x[ranks].rearrange("r t k -> t r k"))
-        raw = []
-        for weights in (w_first, w_second):
-            for r in range(RANKS):
-                shard = keep.tile([P, PACK, WIDTH], BF16, name="raw%d" % len(raw))
-                nc.sync.dma_start(
-                    out=shard[:], in_=weights[r].rearrange("(p t) c -> p t c", t=PACK)
-                )
-                raw.append(shard[:].rearrange("p t (c i) -> p c t i", i=RUN))
+        raw = [keep.tile([P, PACK, WIDTH], BF16, name="raw%d" % s) for s in range(SHARDS)]
+        for r in range(RANKS):
+            nc.sync.dma_start(out=x_rows[:, r, :], in_=x[r])
+            nc.sync.dma_start(out=raw[r][:], in_=w_first[r].rearrange("(p t) c -> p t c", t=PACK))
+        for r in range(RANKS):
+            nc.sync.dma_start(
+                out=raw[RANKS + r][:], in_=w_second[r].rearrange("(p t) c -> p t c", t=PACK)
+            )
+
         grouped = [
             keep.tile([P, WIDTH * PACK], BF16, align_bytes=64, name="grouped%d" % s)
-            for s in range(2 * RANKS)
+            for s in range(SHARDS)
         ]
-        codes = [
-            keep.tile([P, WIDTH], U32, align_bytes=64, name="codes%d" % s)
-            for s in range(2 * RANKS)
-        ]
-        scales = [
-            keep.tile([P, WIDTH], U8, align_bytes=64, name="scales%d" % s)
-            for s in range(2 * RANKS)
-        ]
+        codes = [keep.tile([P, WIDTH], U32, align_bytes=64, name="codes%d" % s) for s in range(SHARDS)]
+        scales = [keep.tile([P, WIDTH], U8, align_bytes=64, name="scales%d" % s) for s in range(SHARDS)]
+        source = []
+        target = []
+        for s in range(SHARDS):
+            runs = raw[s][:].rearrange("p t (c i) -> p c t i", i=RUN)
+            if s < RANKS:
+                places = grouped[s][:].rearrange("p (i c t) -> p c t i", i=RUN, t=PACK)
+                middle = RUN // 2
+                source.append((runs[:, :, :, :middle], runs[:, :, :, middle:]))
+                target.append((places[:, :, :, :middle], places[:, :, :, middle:]))
+            else:
+                places = grouped[s][:].rearrange("p (c i t) -> p c t i", i=RUN, t=PACK)
+                middle = HALF // RUN
+                source.append((runs[:, :middle], runs[:, middle:]))
+                target.append((places[:, :middle], places[:, middle:]))
+
+        def regroup(s):
+            nc.vector.tensor_copy(out=target[s][0], in_=source[s][0])
+            nc.scalar.copy(out=target[s][1], in_=source[s][1])
+
+        def quantise_half(s, h):
+            nc.vector.quantize_mx(
+                out=codes[s][:, h * HALF : (h + 1) * HALF].bitcast(FP8X4),
+                scales=scales[s][:, h * HALF : (h + 1) * HALF],
+                in_=grouped[s][:, h * HALF * PACK : (h + 1) * HALF * PACK],
+            )
 
         identity = keep.tile([P, P], F32)
         make_identity(nc, identity[:])
@@ -73,30 +80,31 @@ def tile_multilayerallreduce_pa_s_kernel(tc, x, w_first, w_second, out):
         )
         x_grouped = keep.tile([P, RANKS * TOKENS * PACK], BF16, align_bytes=64)
         x_grouped_words = x_grouped[:].bitcast(F32).rearrange("p (r c u) -> p r c u", r=RANKS, u=2)
-        for b, engine_copy in enumerate((nc.vector.tensor_copy, nc.scalar.copy)):
-            x_bank = psum.tile([P, BANK_RANKS, 2, TOKENS], F32, name="x_bank%d" % b)
-            for i in range(BANK_RANKS):
-                for u in range(2):
-                    nc.tensor.transpose(
-                        x_bank[:, i, u, :], x_words[:, b * BANK_RANKS + i, u, :], identity[:]
-                    )
-            engine_copy(
-                out=x_grouped_words[:, b * BANK_RANKS : (b + 1) * BANK_RANKS],
-                in_=x_bank[:].rearrange("p r u c -> p r c u"),
-            )
         x_codes = keep.tile([P, RANKS * TOKENS], U32, align_bytes=64)
         x_scales = keep.tile([P, RANKS * TOKENS], U8, align_bytes=64)
+        for r in range(RANKS):
+            x_bank = psum.tile([P, 2, TOKENS], F32, name="x_bank%d" % r)
+            for u in range(2):
+                nc.tensor.transpose(x_bank[:, u, :], x_words[:, r, u, :], identity[:])
+            nc.scalar.copy(out=x_grouped_words[:, r], in_=x_bank[:].rearrange("p u c -> p c u"))
+            regroup(r)
+            if r > 0:
+                quantise_half(r - 1, 1)
+            nc.vector.quantize_mx(
+                out=x_codes[:, r * TOKENS : (r + 1) * TOKENS].bitcast(FP8X4),
+                scales=x_scales[:, r * TOKENS : (r + 1) * TOKENS],
+                in_=x_grouped[:, r * TOKENS * PACK : (r + 1) * TOKENS * PACK],
+            )
+            quantise_half(r, 0)
 
-        for s in range(RANKS):
-            regroup(nc, raw[s], grouped[s][:].rearrange("p (i c t) -> p c t i", i=RUN, t=PACK))
-            if s == 0:
-                quantise(nc, x_grouped[:], x_codes[:], x_scales[:])
-            else:
-                quantise(nc, grouped[s - 1][:], codes[s - 1][:], scales[s - 1][:])
-        quantise(nc, grouped[RANKS - 1][:], codes[RANKS - 1][:], scales[RANKS - 1][:])
+        def second_layer_shard(r):
+            regroup(RANKS + r)
+            quantise_half(RANKS + r - 1, 1)
+            quantise_half(RANKS + r, 0)
 
         hidden_sums = psum.tile([P, PACK, TOKENS], F32)
-        for i in range(PACK):
+
+        def first_layer_group(i):
             for r in range(RANKS):
                 nc.tensor.matmul_mx(
                     out=hidden_sums[:, i, :],
@@ -108,54 +116,52 @@ def tile_multilayerallreduce_pa_s_kernel(tc, x, w_first, w_second, out):
                     stop=(r == RANKS - 1),
                 )
 
-        second = [
-            grouped[RANKS + r][:].rearrange("p (c i t) -> p c t i", i=RUN, t=PACK)
-            for r in range(RANKS)
-        ]
-        last = RANKS - 1
-        for r in range(last):
-            regroup(nc, raw[RANKS + r], second[r])
-            if r > 0:
-                quantise(nc, grouped[RANKS + r - 1][:], codes[RANKS + r - 1][:], scales[RANKS + r - 1][:])
+        first_layer_group(0)
+        first_layer_group(1)
+        second_layer_shard(0)
+        first_layer_group(2)
+        first_layer_group(3)
+        second_layer_shard(1)
 
         hidden_grouped = keep.tile([P, TOKENS, PACK], BF16, align_bytes=64)
         hidden_codes = keep.tile([P, TOKENS], U32, align_bytes=64)
         hidden_scales = keep.tile([P, TOKENS], U8, align_bytes=64)
         nc.scalar.copy(out=hidden_grouped[:], in_=hidden_sums[:].rearrange("p i c -> p c i"))
-        quantise(nc, grouped[RANKS + last - 1][:], codes[RANKS + last - 1][:], scales[RANKS + last - 1][:])
-        quantise(nc, hidden_grouped[:].rearrange("p c i -> p (c i)"), hidden_codes[:], hidden_scales[:])
+        second_layer_shard(2)
+        nc.vector.quantize_mx(
+            out=hidden_codes[:].bitcast(FP8X4),
+            scales=hidden_scales[:],
+            in_=hidden_grouped[:].rearrange("p c i -> p (c i)"),
+        )
 
         total_sums = [psum.tile([TOKENS, HALF], F32, name="total_sums%d" % h) for h in range(2)]
 
         def second_layer_pass(r, h):
-            cols = slice(h * HALF, (h + 1) * HALF)
             nc.tensor.matmul_mx(
                 out=total_sums[h][:],
                 lhsT=hidden_codes[:].bitcast(FP8X4),
                 lhsT_scale=hidden_scales[:],
-                rhs=codes[RANKS + r][:, cols].bitcast(FP8X4),
-                rhs_scale=scales[RANKS + r][:, cols],
+                rhs=codes[RANKS + r][:, h * HALF : (h + 1) * HALF].bitcast(FP8X4),
+                rhs_scale=scales[RANKS + r][:, h * HALF : (h + 1) * HALF],
                 start=(r == 0),
-                stop=(r == last),
+                stop=(r == RANKS - 1),
             )
 
-        for r in range(last):
-            for h in range(2):
-                second_layer_pass(r, h)
-
-        half_runs = HALF // RUN
-        for h in range(2):
-            runs = slice(h * half_runs, (h + 1) * half_runs)
-            regroup(nc, raw[RANKS + last][:, runs], second[last][:, runs])
-        for h, engine_copy in enumerate((nc.scalar.copy, nc.vector.tensor_copy)):
-            quantise(
-                nc,
-                grouped[RANKS + last][:, h * HALF * PACK : (h + 1) * HALF * PACK],
-                codes[RANKS + last][:, h * HALF : (h + 1) * HALF],
-                scales[RANKS + last][:, h * HALF : (h + 1) * HALF],
-            )
-            second_layer_pass(last, h)
+        def store_half(h, engine_copy):
             total = keep.tile([TOKENS, HALF], F32, name="total%d" % h)
             engine_copy(out=total[:], in_=total_sums[h][:])
             for r in range(RANKS):
                 nc.sync.dma_start(out=out[r, :, h * HALF : (h + 1) * HALF], in_=total[:])
+
+        last = RANKS - 1
+        for r in range(last):
+            second_layer_pass(r, 0)
+        for r in range(last - 1):
+            second_layer_pass(r, 1)
+        second_layer_shard(last)
+        second_layer_pass(last - 1, 1)
+        second_layer_pass(last, 0)
+        store_half(0, nc.scalar.copy)
+        quantise_half(SHARDS - 1, 1)
+        second_layer_pass(last, 1)
+        store_half(1, nc.vector.tensor_copy)

@@ -150,8 +150,10 @@ def tile_multilayerallreduce_pa_s_kernel(tc, x, w_first, w_second, out):
         def store_half(h, engine_copy):
             total = keep.tile([TOKENS, HALF], F32, name="total%d" % h)
             engine_copy(out=total[:], in_=total_sums[h][:])
-            for r in range(RANKS):
-                nc.sync.dma_start(out=out[r, :, h * HALF : (h + 1) * HALF], in_=total[:])
+            nc.sync.dma_start(
+                out=out[:, :, h * HALF : (h + 1) * HALF].rearrange("r t c -> t r c"),
+                in_=total[:].unsqueeze(1).to_broadcast([TOKENS, RANKS, HALF]),
+            )
 
         last = RANKS - 1
         for r in range(last):

@@ -116,35 +116,31 @@ def tile_multilayerallreduce_pa_s_kernel(tc, x, w_first, w_second, out):
                     stop=(r == RANKS - 1),
                 )
 
-        first_layer_group(0)
-        first_layer_group(1)
-        second_layer_shard(0)
-        first_layer_group(2)
-        first_layer_group(3)
-        second_layer_shard(1)
+        quantise_half(RANKS - 1, 1)
+        for i in range(PACK):
+            first_layer_group(i)
+        regroup(RANKS)
+        regroup(RANKS + 1)
+        quantise_half(RANKS, 0)
+        quantise_half(RANKS, 1)
+        quantise_half(RANKS + 1, 0)
 
         hidden_grouped = keep.tile([P, TOKENS, PACK], BF16, align_bytes=64)
         hidden_codes = keep.tile([P, TOKENS], U32, align_bytes=64)
         hidden_scales = keep.tile([P, TOKENS], U8, align_bytes=64)
         nc.scalar.copy(out=hidden_grouped[:], in_=hidden_sums[:].rearrange("p i c -> p c i"))
-        second_layer_shard(2)
-        nc.vector.quantize_mx(
-            out=hidden_codes[:].bitcast(FP8X4),
-            scales=hidden_scales[:],
-            in_=hidden_grouped[:].rearrange("p c i -> p (c i)"),
-        )
 
         total_sums = [psum.tile([TOKENS, HALF], F32, name="total_sums%d" % h) for h in range(2)]
 
-        def second_layer_pass(r, h):
+        def second_layer_pass(r, h, start, stop):
             nc.tensor.matmul_mx(
                 out=total_sums[h][:],
                 lhsT=hidden_codes[:].bitcast(FP8X4),
                 lhsT_scale=hidden_scales[:],
                 rhs=codes[RANKS + r][:, h * HALF : (h + 1) * HALF].bitcast(FP8X4),
                 rhs_scale=scales[RANKS + r][:, h * HALF : (h + 1) * HALF],
-                start=(r == 0),
-                stop=(r == RANKS - 1),
+                start=start,
+                stop=stop,
             )
 
         def store_half(h, engine_copy):
@@ -155,15 +151,28 @@ def tile_multilayerallreduce_pa_s_kernel(tc, x, w_first, w_second, out):
                 in_=total[:].unsqueeze(1).to_broadcast([TOKENS, RANKS, HALF]),
             )
 
-        last = RANKS - 1
-        for r in range(last):
-            second_layer_pass(r, 0)
-        for r in range(last - 1):
-            second_layer_pass(r, 1)
-        second_layer_shard(last)
-        second_layer_pass(last - 1, 1)
-        second_layer_pass(last, 0)
+        nc.vector.quantize_mx(
+            out=hidden_codes[:].bitcast(FP8X4),
+            scales=hidden_scales[:],
+            in_=hidden_grouped[:].rearrange("p c i -> p (c i)"),
+        )
+        quantise_half(RANKS + 1, 1)
+        s2 = RANKS + 2
+        s3 = RANKS + 3
+        nc.scalar.copy(out=target[s2][0], in_=source[s2][0])
+        nc.vector.tensor_copy(out=target[s3][0], in_=source[s3][0])
+        quantise_half(s2, 0)
+        quantise_half(s3, 0)
+        nc.scalar.copy(out=target[s2][1], in_=source[s2][1])
+        nc.vector.tensor_copy(out=target[s3][1], in_=source[s3][1])
+        for h in range(2):
+            second_layer_pass(0, h, True, False)
+            second_layer_pass(1, h, False, False)
+        second_layer_pass(2, 0, False, False)
+        second_layer_pass(3, 0, False, True)
         store_half(0, nc.scalar.copy)
-        quantise_half(SHARDS - 1, 1)
-        second_layer_pass(last, 1)
+        quantise_half(s2, 1)
+        second_layer_pass(2, 1, False, False)
+        quantise_half(s3, 1)
+        second_layer_pass(3, 1, False, True)
         store_half(1, nc.vector.tensor_copy)

@@ -82,6 +82,20 @@ def tile_multilayerallreduce_pa_s_kernel(tc, x, w_first, w_second, out):
         x_grouped_words = x_grouped[:].bitcast(F32).rearrange("p (r c u) -> p r c u", r=RANKS, u=2)
         x_codes = keep.tile([P, RANKS * TOKENS], U32, align_bytes=64)
         x_scales = keep.tile([P, RANKS * TOKENS], U8, align_bytes=64)
+        idle_sums = psum.tile([TOKENS, WIDTH], F32)
+
+        def keep_busy(passes):
+            for e in range(passes):
+                nc.tensor.matmul_mx(
+                    out=idle_sums[:],
+                    lhsT=x_codes[:, :TOKENS].bitcast(FP8X4),
+                    lhsT_scale=x_scales[:, :TOKENS],
+                    rhs=codes[0][:].bitcast(FP8X4),
+                    rhs_scale=scales[0][:],
+                    start=True,
+                    stop=True,
+                )
+
         for r in range(RANKS):
             x_bank = psum.tile([P, 2, TOKENS], F32, name="x_bank%d" % r)
             for u in range(2):
@@ -96,6 +110,8 @@ def tile_multilayerallreduce_pa_s_kernel(tc, x, w_first, w_second, out):
                 in_=x_grouped[:, r * TOKENS * PACK : (r + 1) * TOKENS * PACK],
             )
             quantise_half(r, 0)
+            if r == 2:
+                keep_busy(2)
 
         def second_layer_shard(r):
             regroup(RANKS + r)
@@ -106,6 +122,8 @@ def tile_multilayerallreduce_pa_s_kernel(tc, x, w_first, w_second, out):
 
         def first_layer_group(i):
             for r in range(RANKS):
+                if i == 0 and r >= 2:
+                    keep_busy(2)
                 nc.tensor.matmul_mx(
                     out=hidden_sums[:, i, :],
                     lhsT=codes[r][:, i * P : (i + 1) * P].bitcast(FP8X4),
@@ -119,6 +137,7 @@ def tile_multilayerallreduce_pa_s_kernel(tc, x, w_first, w_second, out):
         quantise_half(RANKS - 1, 1)
         for i in range(PACK):
             first_layer_group(i)
+        keep_busy(2)
         regroup(RANKS)
         regroup(RANKS + 1)
         quantise_half(RANKS, 0)
@@ -170,6 +189,7 @@ def tile_multilayerallreduce_pa_s_kernel(tc, x, w_first, w_second, out):
             second_layer_pass(1, h, False, False)
         second_layer_pass(2, 0, False, False)
         second_layer_pass(3, 0, False, True)
+        keep_busy(2)
         store_half(0, nc.scalar.copy)
         quantise_half(s2, 1)
         second_layer_pass(2, 1, False, False)

@@ -18,6 +18,8 @@ TOKENS = 128
 WIDTH = 512
 HALF = WIDTH // 2
 
+VECTOR_COLUMNS = 304
+
 FLOPS = 2 * 2 * RANKS * TOKENS * WIDTH * WIDTH
 
 
@@ -55,7 +57,7 @@ def tile_multilayerallreduce_pa_s_kernel(tc, x, w_first, w_second, out):
                 target.append((places[:, :, :, :middle], places[:, :, :, middle:]))
             else:
                 places = grouped[s][:].rearrange("p (c i t) -> p c t i", i=RUN, t=PACK)
-                middle = HALF // RUN
+                middle = (VECTOR_COLUMNS if s < RANKS + 2 else HALF) // RUN
                 source.append((runs[:, :middle], runs[:, middle:]))
                 target.append((places[:, :middle], places[:, middle:]))
 

@@ -112,8 +112,6 @@ def tile_multilayerallreduce_pa_s_kernel(tc, x, w_first, w_second, out):
                 in_=x_grouped[:, r * TOKENS * PACK : (r + 1) * TOKENS * PACK],
             )
             quantise_half(r, 0)
-            if r == 2:
-                keep_busy(2)
 
         def second_layer_shard(r):
             regroup(RANKS + r)
@@ -139,7 +137,6 @@ def tile_multilayerallreduce_pa_s_kernel(tc, x, w_first, w_second, out):
         quantise_half(RANKS - 1, 1)
         for i in range(PACK):
             first_layer_group(i)
-        keep_busy(2)
         regroup(RANKS)
         regroup(RANKS + 1)
         quantise_half(RANKS, 0)
@@ -191,7 +188,6 @@ def tile_multilayerallreduce_pa_s_kernel(tc, x, w_first, w_second, out):
             second_layer_pass(1, h, False, False)
         second_layer_pass(2, 0, False, False)
         second_layer_pass(3, 0, False, True)
-        keep_busy(2)
         store_half(0, nc.scalar.copy)
         quantise_half(s2, 1)
         second_layer_pass(2, 1, False, False)

@@ -36,9 +36,13 @@ def tile_multilayerallreduce_pa_s_kernel(tc, x, w_first, w_second, out):
             nc.sync.dma_start(out=x_rows[:, r, :], in_=x[r])
             nc.sync.dma_start(out=raw[r][:], in_=w_first[r].rearrange("(p t) c -> p t c", t=PACK))
         for r in range(RANKS):
-            nc.sync.dma_start(
-                out=raw[RANKS + r][:], in_=w_second[r].rearrange("(p t) c -> p t c", t=PACK)
-            )
+            for columns in (
+                [slice(0, HALF), slice(HALF, WIDTH)] if r == RANKS - 1 else [slice(0, WIDTH)]
+            ):
+                nc.sync.dma_start(
+                    out=raw[RANKS + r][:, :, columns],
+                    in_=w_second[r][:, columns].rearrange("(p t) c -> p t c", t=PACK),
+                )
 
         grouped = [
             keep.tile([P, WIDTH * PACK], BF16, align_bytes=64, name="grouped%d" % s)

@@ -13,7 +13,6 @@ P = 128
 PACK = 4
 RUN = 4
 RANKS = 4
-SHARDS = 2 * RANKS
 TOKENS = 128
 WIDTH = 512
 HALF = WIDTH // 2
@@ -31,53 +30,79 @@ def tile_multilayerallreduce_pa_s_kernel(tc, x, w_first, w_second, out):
         ctx.enter_context(tc.manual_schedule())
 
         x_rows = keep.tile([TOKENS, RANKS, WIDTH], BF16)
-        raw = [keep.tile([P, PACK, WIDTH], BF16, name="raw%d" % s) for s in range(SHARDS)]
-        for r in range(RANKS):
-            nc.sync.dma_start(out=x_rows[:, r, :], in_=x[r])
-            nc.sync.dma_start(out=raw[r][:], in_=w_first[r].rearrange("(p t) c -> p t c", t=PACK))
-        for r in range(RANKS):
-            for columns in (
-                [slice(0, HALF), slice(HALF, WIDTH)] if r == RANKS - 1 else [slice(0, WIDTH)]
-            ):
-                nc.sync.dma_start(
-                    out=raw[RANKS + r][:, :, columns],
-                    in_=w_second[r][:, columns].rearrange("(p t) c -> p t c", t=PACK),
-                )
+        raw = [keep.tile([P, PACK, WIDTH], BF16, name="raw%d" % s) for s in range(2 * RANKS)]
 
-        grouped = [
-            keep.tile([P, WIDTH * PACK], BF16, align_bytes=64, name="grouped%d" % s)
-            for s in range(SHARDS)
-        ]
-        codes = [keep.tile([P, WIDTH], U32, align_bytes=64, name="codes%d" % s) for s in range(SHARDS)]
-        scales = [keep.tile([P, WIDTH], U8, align_bytes=64, name="scales%d" % s) for s in range(SHARDS)]
-        source = []
-        target = []
-        for s in range(SHARDS):
-            runs = raw[s][:].rearrange("p t (c i) -> p c t i", i=RUN)
-            if s < RANKS:
-                places = grouped[s][:].rearrange("p (i c t) -> p c t i", i=RUN, t=PACK)
-                middle = RUN // 2
-                source.append((runs[:, :, :, :middle], runs[:, :, :, middle:]))
-                target.append((places[:, :, :, :middle], places[:, :, :, middle:]))
-            else:
-                places = grouped[s][:].rearrange("p (c i t) -> p c t i", i=RUN, t=PACK)
-                middle = (VECTOR_COLUMNS if s < RANKS + 2 else HALF) // RUN
-                source.append((runs[:, :middle], runs[:, middle:]))
-                target.append((places[:, :middle], places[:, middle:]))
+        def load_weights(s):
+            w = w_first[s] if s < RANKS else w_second[s - RANKS]
+            nc.sync.dma_start(out=raw[s][:], in_=w.rearrange("(p t) c -> p t c", t=PACK))
 
-        def regroup(s):
-            nc.vector.tensor_copy(out=target[s][0], in_=source[s][0])
-            nc.scalar.copy(out=target[s][1], in_=source[s][1])
-
-        def quantise_half(s, h):
-            nc.vector.quantize_mx(
-                out=codes[s][:, h * HALF : (h + 1) * HALF].bitcast(FP8X4),
-                scales=scales[s][:, h * HALF : (h + 1) * HALF],
-                in_=grouped[s][:, h * HALF * PACK : (h + 1) * HALF * PACK],
+        def load_columns(s, c0, c1):
+            w = w_first[s] if s < RANKS else w_second[s - RANKS]
+            nc.sync.dma_start(
+                out=raw[s][:, :, c0:c1], in_=w[:, c0:c1].rearrange("(p t) c -> p t c", t=PACK)
             )
+
+        def load_x(r0, n):
+            nc.sync.dma_start(
+                out=x_rows[:, r0 : r0 + n, :], in_=x[r0 : r0 + n].rearrange("r t k -> t r k")
+            )
+
+        for r in range(RANKS):
+            load_x(r, 1)
+            load_weights(r)
+        load_weights(RANKS + 0)
+        load_weights(RANKS + 1)
+        load_weights(RANKS + 2)
+        load_columns(RANKS + 3, 0, HALF)
+        load_columns(RANKS + 3, HALF, WIDTH)
+
+        grouped = [keep.tile([P, RANKS * WIDTH * PACK], BF16, align_bytes=64, name="grouped%d" % l) for l in range(2)]
+        codes = [keep.tile([P, RANKS * WIDTH], U32, align_bytes=64, name="codes%d" % l) for l in range(2)]
+        scales = [keep.tile([P, RANKS * WIDTH], U8, align_bytes=64, name="scales%d" % l) for l in range(2)]
+
+        def quantise(layer, c0, n):
+            nc.vector.quantize_mx(
+                out=codes[layer][:, c0 : c0 + n].bitcast(FP8X4),
+                scales=scales[layer][:, c0 : c0 + n],
+                in_=grouped[layer][:, c0 * PACK : (c0 + n) * PACK],
+            )
+
+        def first_views(r, i0, i1):
+            src = raw[r][:].rearrange("p t (c i) -> p c t i", i=RUN)
+            dst = grouped[0][:, r * WIDTH * PACK : (r + 1) * WIDTH * PACK].rearrange(
+                "p (i c t) -> p c t i", i=RUN, t=PACK
+            )
+            return dst[:, :, :, i0:i1], src[:, :, :, i0:i1]
+
+        pieces = [(0, HALF), (HALF, P), (HALF + P, P)]
+
+        def place(r, c):
+            for c0, n in pieces:
+                if c < c0 + n:
+                    return c0 * RANKS + r * n + c - c0
+
+        def first_part(r, i0, i1, a, b):
+            dst, src = first_views(r, i0, i1)
+            return dst[:, a:b], src[:, a:b]
+
+        def second_views(r, c0, c1):
+            src = raw[RANKS + r][:, :, c0:c1].rearrange("p t (c i) -> p c t i", i=RUN)
+            m0 = place(r, c0) * PACK
+            dst = grouped[1][:, m0 : m0 + (c1 - c0) * PACK].rearrange(
+                "p (c i t) -> p c t i", i=RUN, t=PACK
+            )
+            return dst, src
+
+        def vcopy(views):
+            nc.vector.tensor_copy(out=views[0], in_=views[1])
+
+        def scopy(views):
+            nc.scalar.copy(out=views[0], in_=views[1])
 
         identity = keep.tile([P, P], F32)
         make_identity(nc, identity[:])
+        identity_bf16 = keep.tile([P, P], BF16)
+        make_identity(nc, identity_bf16[:])
         x_words = (
             x_rows[:]
             .rearrange("t r k -> t (r k)")
@@ -88,113 +113,164 @@ def tile_multilayerallreduce_pa_s_kernel(tc, x, w_first, w_second, out):
         x_grouped_words = x_grouped[:].bitcast(F32).rearrange("p (r c u) -> p r c u", r=RANKS, u=2)
         x_codes = keep.tile([P, RANKS * TOKENS], U32, align_bytes=64)
         x_scales = keep.tile([P, RANKS * TOKENS], U8, align_bytes=64)
-        idle_sums = psum.tile([TOKENS, WIDTH], F32)
+        idle_sums = psum.tile([TOKENS, WIDTH], F32, name="idle_sums")
 
         def keep_busy(passes):
             for e in range(passes):
                 nc.tensor.matmul_mx(
                     out=idle_sums[:],
-                    lhsT=x_codes[:, :TOKENS].bitcast(FP8X4),
-                    lhsT_scale=x_scales[:, :TOKENS],
-                    rhs=codes[0][:].bitcast(FP8X4),
-                    rhs_scale=scales[0][:],
+                    lhsT=codes[0][:, :P].bitcast(FP8X4),
+                    lhsT_scale=scales[0][:, :P],
+                    rhs=codes[0][:, :WIDTH].bitcast(FP8X4),
+                    rhs_scale=scales[0][:, :WIDTH],
                     start=True,
                     stop=True,
                 )
 
-        for r in range(RANKS):
-            x_bank = psum.tile([P, 2, TOKENS], F32, name="x_bank%d" % r)
-            for u in range(2):
-                nc.tensor.transpose(x_bank[:, u, :], x_words[:, r, u, :], identity[:])
-            nc.scalar.copy(out=x_grouped_words[:, r], in_=x_bank[:].rearrange("p u c -> p c u"))
-            regroup(r)
-            if r > 0:
-                quantise_half(r - 1, 1)
-            nc.vector.quantize_mx(
-                out=x_codes[:, r * TOKENS : (r + 1) * TOKENS].bitcast(FP8X4),
-                scales=x_scales[:, r * TOKENS : (r + 1) * TOKENS],
-                in_=x_grouped[:, r * TOKENS * PACK : (r + 1) * TOKENS * PACK],
+        def x_out(r0, n):
+            bank = psum.tile([P, n, 2, TOKENS], F32, name="x_bank%d" % r0)
+            for r in range(n):
+                for u in range(2):
+                    nc.tensor.transpose(bank[:, r, u, :], x_words[:, r0 + r, u, :], identity[:])
+            nc.scalar.copy(
+                out=x_grouped_words[:, r0 : r0 + n], in_=bank[:].rearrange("p r u c -> p r c u")
             )
-            quantise_half(r, 0)
 
-        def second_layer_shard(r):
-            regroup(RANKS + r)
-            quantise_half(RANKS + r - 1, 1)
-            quantise_half(RANKS + r, 0)
+        def x_quant(r0, n):
+            nc.vector.quantize_mx(
+                out=x_codes[:, r0 * TOKENS : (r0 + n) * TOKENS].bitcast(FP8X4),
+                scales=x_scales[:, r0 * TOKENS : (r0 + n) * TOKENS],
+                in_=x_grouped[:, r0 * TOKENS * PACK : (r0 + n) * TOKENS * PACK],
+            )
 
         hidden_sums = psum.tile([P, PACK, TOKENS], F32)
 
-        def first_layer_group(i):
-            for r in range(RANKS):
-                if i == 0 and r >= 2:
-                    keep_busy(2)
-                nc.tensor.matmul_mx(
-                    out=hidden_sums[:, i, :],
-                    lhsT=codes[r][:, i * P : (i + 1) * P].bitcast(FP8X4),
-                    lhsT_scale=scales[r][:, i * P : (i + 1) * P],
-                    rhs=x_codes[:, r * TOKENS : (r + 1) * TOKENS].bitcast(FP8X4),
-                    rhs_scale=x_scales[:, r * TOKENS : (r + 1) * TOKENS],
-                    start=(r == 0),
-                    stop=(r == RANKS - 1),
-                )
-
-        quantise_half(RANKS - 1, 1)
-        for i in range(PACK):
-            first_layer_group(i)
-        regroup(RANKS)
-        regroup(RANKS + 1)
-        quantise_half(RANKS, 0)
-        quantise_half(RANKS, 1)
-        quantise_half(RANKS + 1, 0)
+        def first_layer_pass(i, r):
+            c0 = r * WIDTH + i * P
+            nc.tensor.matmul_mx(
+                out=hidden_sums[:, i, :],
+                lhsT=codes[0][:, c0 : c0 + P].bitcast(FP8X4),
+                lhsT_scale=scales[0][:, c0 : c0 + P],
+                rhs=x_codes[:, r * TOKENS : (r + 1) * TOKENS].bitcast(FP8X4),
+                rhs_scale=x_scales[:, r * TOKENS : (r + 1) * TOKENS],
+                start=(r == 0),
+                stop=(r == RANKS - 1),
+            )
 
         hidden_grouped = keep.tile([P, TOKENS, PACK], BF16, align_bytes=64)
         hidden_codes = keep.tile([P, TOKENS], U32, align_bytes=64)
         hidden_scales = keep.tile([P, TOKENS], U8, align_bytes=64)
-        nc.scalar.copy(out=hidden_grouped[:], in_=hidden_sums[:].rearrange("p i c -> p c i"))
 
-        total_sums = [psum.tile([TOKENS, HALF], F32, name="total_sums%d" % h) for h in range(2)]
+        total_sums = []
+        totals = [keep.tile([TOKENS, n], F32, name="total_sb%d" % c0) for c0, n in pieces]
 
-        def second_layer_pass(r, h, start, stop):
+        def second_layer_pass(r, k, start, stop):
+            c0, n = pieces[k]
+            m0 = place(r, c0)
             nc.tensor.matmul_mx(
-                out=total_sums[h][:],
+                out=total_sums[k][:, :n],
                 lhsT=hidden_codes[:].bitcast(FP8X4),
                 lhsT_scale=hidden_scales[:],
-                rhs=codes[RANKS + r][:, h * HALF : (h + 1) * HALF].bitcast(FP8X4),
-                rhs_scale=scales[RANKS + r][:, h * HALF : (h + 1) * HALF],
+                rhs=codes[1][:, m0 : m0 + n].bitcast(FP8X4),
+                rhs_scale=scales[1][:, m0 : m0 + n],
                 start=start,
                 stop=stop,
             )
 
-        def store_half(h, engine_copy):
-            total = keep.tile([TOKENS, HALF], F32, name="total%d" % h)
-            engine_copy(out=total[:], in_=total_sums[h][:])
+        def store(k, engine_copy):
+            c0, n = pieces[k]
+            engine_copy(out=totals[k][:], in_=total_sums[k][:, :n])
             nc.sync.dma_start(
-                out=out[:, :, h * HALF : (h + 1) * HALF].rearrange("r t c -> t r c"),
-                in_=total[:].unsqueeze(1).to_broadcast([TOKENS, RANKS, HALF]),
+                out=out[:, :, c0 : c0 + n].rearrange("r t c -> t r c"),
+                in_=totals[k][:].unsqueeze(1).to_broadcast([TOKENS, RANKS, n]),
             )
 
-        nc.vector.quantize_mx(
-            out=hidden_codes[:].bitcast(FP8X4),
-            scales=hidden_scales[:],
-            in_=hidden_grouped[:].rearrange("p c i -> p (c i)"),
-        )
-        quantise_half(RANKS + 1, 1)
-        s2 = RANKS + 2
-        s3 = RANKS + 3
-        nc.scalar.copy(out=target[s2][0], in_=source[s2][0])
-        nc.vector.tensor_copy(out=target[s3][0], in_=source[s3][0])
-        quantise_half(s2, 0)
-        quantise_half(s3, 0)
-        nc.scalar.copy(out=target[s2][1], in_=source[s2][1])
-        nc.vector.tensor_copy(out=target[s3][1], in_=source[s3][1])
-        for h in range(2):
-            second_layer_pass(0, h, True, False)
-            second_layer_pass(1, h, False, False)
-        second_layer_pass(2, 0, False, False)
-        second_layer_pass(3, 0, False, True)
-        store_half(0, nc.scalar.copy)
-        quantise_half(s2, 1)
-        second_layer_pass(2, 1, False, False)
-        quantise_half(s3, 1)
-        second_layer_pass(3, 1, False, True)
-        store_half(1, nc.vector.tensor_copy)
+        def hidden_copy():
+            nc.scalar.copy(out=hidden_grouped[:], in_=hidden_sums[:].rearrange("p i c -> p c i"))
+
+        def hidden_quant():
+            nc.vector.quantize_mx(
+                out=hidden_codes[:].bitcast(FP8X4),
+                scales=hidden_scales[:],
+                in_=hidden_grouped[:].rearrange("p c i -> p (c i)"),
+            )
+
+        regrouped = {}
+
+        def by_identity(r, quarter, bank, q):
+            if bank not in regrouped:
+                regrouped[bank] = psum.tile([P, 2 * WIDTH], BF16, name=bank)
+            nc.tensor.matmul(
+                out=regrouped[bank][:, q * WIDTH : (q + 1) * WIDTH],
+                lhsT=identity_bf16[:],
+                rhs=raw[RANKS + r][:, :, quarter * P : (quarter + 1) * P].rearrange("p t c -> p c t"),
+                start=True,
+                stop=True,
+            )
+
+        def identity_copy(r, quarter, bank, q, n):
+            c0 = place(r, quarter * P)
+            nc.scalar.copy(
+                out=grouped[1][:, c0 * PACK : (c0 + n * P) * PACK],
+                in_=regrouped[bank][:, q * WIDTH : (q + n) * WIDTH],
+            )
+
+        for r in range(RANKS):
+            x_out(r, 1)
+            vcopy(first_views(r, 0, 2))
+            scopy(first_views(r, 2, 4))
+            if r > 0:
+                quantise(0, (r - 1) * WIDTH + HALF, HALF)
+            x_quant(r, 1)
+            quantise(0, r * WIDTH, HALF)
+        q = lambda r, i: second_views(r, i * P, (i + 1) * P)
+        scopy(q(0, 2))
+        scopy(q(0, 3))
+        vcopy(second_views(0, 0, HALF))
+        quantise(0, 3 * WIDTH + HALF, HALF)
+        for i in range(PACK):
+            for r in range(RANKS):
+                if i == 0 and r == 2:
+                    keep_busy(2)
+                if i == 0 and r == 3:
+                    keep_busy(2)
+                first_layer_pass(i, r)
+        total_sums += [
+            psum.tile([TOKENS, WIDTH], F32, name=name) for name in ("total0", "total1", "idle_sums")
+        ]
+        quantise(1, 0, HALF)
+        vcopy(second_views(1, 0, HALF))
+        scopy(q(1, 2))
+        scopy(q(1, 3))
+        quantise(1, HALF, HALF)
+        vcopy(second_views(2, 0, HALF))
+
+        hidden_copy()
+        scopy(second_views(3, 128, HALF))
+
+
+        vcopy(second_views(3, 0, 128))
+        hidden_quant()
+        quantise(1, 2 * HALF, HALF)
+
+        quantise(1, 3 * HALF, HALF)
+        scopy(q(2, 2))
+        for r in range(RANKS):
+            second_layer_pass(r, 0, r == 0, r == 3)
+
+        store(0, nc.scalar.copy)
+        scopy(q(2, 3))
+        vcopy(q(3, 2))
+        quantise(1, 4 * HALF, 2 * P)
+        quantise(1, 4 * HALF + 2 * P, 2 * P)
+        vcopy(q(3, 3))
+        for r in range(RANKS):
+            second_layer_pass(r, 1, r == 0, r == 3)
+        quantise(1, 6 * HALF, 2 * P)
+        second_layer_pass(0, 2, True, False)
+        second_layer_pass(1, 2, False, False)
+        store(1, nc.scalar.copy)
+        quantise(1, 6 * HALF + 2 * P, 2 * P)
+        second_layer_pass(2, 2, False, False)
+        second_layer_pass(3, 2, False, True)
+        store(2, nc.scalar.copy)

@@ -233,37 +233,34 @@ def tile_multilayerallreduce_pa_s_kernel(tc, x, w_first, w_second, out):
                 if i == 0 and r == 2:
                     keep_busy(2)
                 if i == 0 and r == 3:
-                    keep_busy(2)
+                    keep_busy(0)
                 first_layer_pass(i, r)
+        vcopy(second_views(1, 0, HALF))
+        scopy(q(1, 2))
+        hidden_copy()
+        scopy(q(1, 3))
+        keep_busy(2)
         total_sums += [
             psum.tile([TOKENS, WIDTH], F32, name=name) for name in ("total0", "total1", "idle_sums")
         ]
         quantise(1, 0, HALF)
-        vcopy(second_views(1, 0, HALF))
-        scopy(q(1, 2))
-        scopy(q(1, 3))
         quantise(1, HALF, HALF)
         vcopy(second_views(2, 0, HALF))
-
-        hidden_copy()
-        scopy(second_views(3, 128, HALF))
-
-
-        vcopy(second_views(3, 0, 128))
         hidden_quant()
+        vcopy(second_views(3, 0, 160))
         quantise(1, 2 * HALF, HALF)
-
-        quantise(1, 3 * HALF, HALF)
+        scopy(second_views(3, 160, HALF))
+        scopy(q(2, 3))
         scopy(q(2, 2))
+        quantise(1, 3 * HALF, HALF)
         for r in range(RANKS):
             second_layer_pass(r, 0, r == 0, r == 3)
-
         store(0, nc.scalar.copy)
-        scopy(q(2, 3))
+
         vcopy(q(3, 2))
         quantise(1, 4 * HALF, 2 * P)
-        quantise(1, 4 * HALF + 2 * P, 2 * P)
         vcopy(q(3, 3))
+        quantise(1, 4 * HALF + 2 * P, 2 * P)
         for r in range(RANKS):
             second_layer_pass(r, 1, r == 0, r == 3)
         quantise(1, 6 * HALF, 2 * P)
@@ -273,4 +270,4 @@ def tile_multilayerallreduce_pa_s_kernel(tc, x, w_first, w_second, out):
         quantise(1, 6 * HALF + 2 * P, 2 * P)
         second_layer_pass(2, 2, False, False)
         second_layer_pass(3, 2, False, True)
-        store(2, nc.scalar.copy)
+        store(2, nc.vector.tensor_copy)

@@ -266,8 +266,13 @@ def tile_multilayerallreduce_pa_s_kernel(tc, x, w_first, w_second, out):
         quantise(1, 6 * HALF, 2 * P)
         second_layer_pass(0, 2, True, False)
         second_layer_pass(1, 2, False, False)
-        store(1, nc.scalar.copy)
+        last = keep.tile([TOKENS, HALF], F32)
+        nc.scalar.copy(out=last[:, :P], in_=total_sums[1][:, :P])
         quantise(1, 6 * HALF + 2 * P, 2 * P)
         second_layer_pass(2, 2, False, False)
         second_layer_pass(3, 2, False, True)
-        store(2, nc.vector.tensor_copy)
+        nc.vector.tensor_copy(out=last[:, P:], in_=total_sums[2][:, :P])
+        nc.sync.dma_start(
+            out=out[:, :, HALF:].rearrange("r t c -> t r c"),
+            in_=last[:].unsqueeze(1).to_broadcast([TOKENS, RANKS, HALF]),
+        )

@@ -226,7 +226,6 @@ def tile_multilayerallreduce_pa_s_kernel(tc, x, w_first, w_second, out):
         q = lambda r, i: second_views(r, i * P, (i + 1) * P)
         scopy(q(0, 2))
         scopy(q(0, 3))
-        vcopy(second_views(0, 0, HALF))
         quantise(0, 3 * WIDTH + HALF, HALF)
         for i in range(PACK):
             for r in range(RANKS):
@@ -235,11 +234,12 @@ def tile_multilayerallreduce_pa_s_kernel(tc, x, w_first, w_second, out):
                 if i == 0 and r == 3:
                     keep_busy(0)
                 first_layer_pass(i, r)
+        vcopy(second_views(0, 0, HALF))
         vcopy(second_views(1, 0, HALF))
         scopy(q(1, 2))
         hidden_copy()
-        scopy(q(1, 3))
-        keep_busy(2)
+        by_identity(1, 3, "x_bank0", 0)
+        by_identity(2, 3, "x_bank0", 1)
         total_sums += [
             psum.tile([TOKENS, WIDTH], F32, name=name) for name in ("total0", "total1", "idle_sums")
         ]
@@ -249,9 +249,11 @@ def tile_multilayerallreduce_pa_s_kernel(tc, x, w_first, w_second, out):
         hidden_quant()
         vcopy(second_views(3, 0, 160))
         quantise(1, 2 * HALF, HALF)
-        scopy(second_views(3, 160, HALF))
-        scopy(q(2, 3))
         scopy(q(2, 2))
+        scopy(second_views(3, 160, HALF))
+
+        identity_copy(1, 3, "x_bank0", 0, 2)
+        scopy(second_views(3, 384, WIDTH))
         quantise(1, 3 * HALF, HALF)
         for r in range(RANKS):
             second_layer_pass(r, 0, r == 0, r == 3)
@@ -259,7 +261,7 @@ def tile_multilayerallreduce_pa_s_kernel(tc, x, w_first, w_second, out):
 
         vcopy(q(3, 2))
         quantise(1, 4 * HALF, 2 * P)
-        vcopy(q(3, 3))
+
         quantise(1, 4 * HALF + 2 * P, 2 * P)
         for r in range(RANKS):
             second_layer_pass(r, 1, r == 0, r == 3)

@@ -16,8 +16,12 @@ RANKS = 4
 TOKENS = 128
 WIDTH = 512
 HALF = WIDTH // 2
+QUARTER = WIDTH // 4
+LAST = RANKS - 1
 
-VECTOR_COLUMNS = 304
+PIECES = ((0, HALF), (HALF, QUARTER), (HALF + QUARTER, QUARTER))
+
+LAST_SHARD_VECTOR_COLUMNS = 160
 
 FLOPS = 2 * 2 * RANKS * TOKENS * WIDTH * WIDTH
 
@@ -30,74 +34,51 @@ def tile_multilayerallreduce_pa_s_kernel(tc, x, w_first, w_second, out):
         ctx.enter_context(tc.manual_schedule())
 
         x_rows = keep.tile([TOKENS, RANKS, WIDTH], BF16)
-        raw = [keep.tile([P, PACK, WIDTH], BF16, name="raw%d" % s) for s in range(2 * RANKS)]
+        raw_first = [keep.tile([P, PACK, WIDTH], BF16, name="raw_first%d" % r) for r in range(RANKS)]
+        raw_second = [keep.tile([P, PACK, WIDTH], BF16, name="raw_second%d" % r) for r in range(RANKS)]
 
-        def load_weights(s):
-            w = w_first[s] if s < RANKS else w_second[s - RANKS]
-            nc.sync.dma_start(out=raw[s][:], in_=w.rearrange("(p t) c -> p t c", t=PACK))
-
-        def load_columns(s, c0, c1):
-            w = w_first[s] if s < RANKS else w_second[s - RANKS]
+        def load_columns(raw, weights, c0, c1):
             nc.sync.dma_start(
-                out=raw[s][:, :, c0:c1], in_=w[:, c0:c1].rearrange("(p t) c -> p t c", t=PACK)
-            )
-
-        def load_x(r0, n):
-            nc.sync.dma_start(
-                out=x_rows[:, r0 : r0 + n, :], in_=x[r0 : r0 + n].rearrange("r t k -> t r k")
+                out=raw[:, :, c0:c1], in_=weights[:, c0:c1].rearrange("(p t) c -> p t c", t=PACK)
             )
 
         for r in range(RANKS):
-            load_x(r, 1)
-            load_weights(r)
-        load_weights(RANKS + 0)
-        load_weights(RANKS + 1)
-        load_weights(RANKS + 2)
-        load_columns(RANKS + 3, 0, HALF)
-        load_columns(RANKS + 3, HALF, WIDTH)
+            nc.sync.dma_start(out=x_rows[:, r, :], in_=x[r])
+            load_columns(raw_first[r], w_first[r], 0, WIDTH)
+        for r in range(LAST):
+            load_columns(raw_second[r], w_second[r], 0, WIDTH)
+        load_columns(raw_second[LAST], w_second[LAST], 0, HALF)
+        load_columns(raw_second[LAST], w_second[LAST], HALF, WIDTH)
 
-        grouped = [keep.tile([P, RANKS * WIDTH * PACK], BF16, align_bytes=64, name="grouped%d" % l) for l in range(2)]
-        codes = [keep.tile([P, RANKS * WIDTH], U32, align_bytes=64, name="codes%d" % l) for l in range(2)]
-        scales = [keep.tile([P, RANKS * WIDTH], U8, align_bytes=64, name="scales%d" % l) for l in range(2)]
+        def operand_tiles(layer):
+            return (
+                keep.tile([P, RANKS * WIDTH * PACK], BF16, align_bytes=64, name="grouped_" + layer),
+                keep.tile([P, RANKS * WIDTH], U32, align_bytes=64, name="codes_" + layer),
+                keep.tile([P, RANKS * WIDTH], U8, align_bytes=64, name="scales_" + layer),
+            )
 
-        def quantise(layer, c0, n):
+        first = operand_tiles("first")
+        second = operand_tiles("second")
+
+        def quantise(tiles, place, columns):
+            grouped, codes, scales = tiles
             nc.vector.quantize_mx(
-                out=codes[layer][:, c0 : c0 + n].bitcast(FP8X4),
-                scales=scales[layer][:, c0 : c0 + n],
-                in_=grouped[layer][:, c0 * PACK : (c0 + n) * PACK],
+                out=codes[:, place : place + columns].bitcast(FP8X4),
+                scales=scales[:, place : place + columns],
+                in_=grouped[:, place * PACK : (place + columns) * PACK],
             )
 
-        def first_views(r, i0, i1):
-            src = raw[r][:].rearrange("p t (c i) -> p c t i", i=RUN)
-            dst = grouped[0][:, r * WIDTH * PACK : (r + 1) * WIDTH * PACK].rearrange(
-                "p (i c t) -> p c t i", i=RUN, t=PACK
+        def mx_pass(acc, stationary, moving, start, stop):
+            (lc, ls, l0, ln), (rc, rs, r0, rn) = stationary, moving
+            nc.tensor.matmul_mx(
+                out=acc,
+                lhsT=lc[:, l0 : l0 + ln].bitcast(FP8X4),
+                lhsT_scale=ls[:, l0 : l0 + ln],
+                rhs=rc[:, r0 : r0 + rn].bitcast(FP8X4),
+                rhs_scale=rs[:, r0 : r0 + rn],
+                start=start,
+                stop=stop,
             )
-            return dst[:, :, :, i0:i1], src[:, :, :, i0:i1]
-
-        pieces = [(0, HALF), (HALF, P), (HALF + P, P)]
-
-        def place(r, c):
-            for c0, n in pieces:
-                if c < c0 + n:
-                    return c0 * RANKS + r * n + c - c0
-
-        def first_part(r, i0, i1, a, b):
-            dst, src = first_views(r, i0, i1)
-            return dst[:, a:b], src[:, a:b]
-
-        def second_views(r, c0, c1):
-            src = raw[RANKS + r][:, :, c0:c1].rearrange("p t (c i) -> p c t i", i=RUN)
-            m0 = place(r, c0) * PACK
-            dst = grouped[1][:, m0 : m0 + (c1 - c0) * PACK].rearrange(
-                "p (c i t) -> p c t i", i=RUN, t=PACK
-            )
-            return dst, src
-
-        def vcopy(views):
-            nc.vector.tensor_copy(out=views[0], in_=views[1])
-
-        def scopy(views):
-            nc.scalar.copy(out=views[0], in_=views[1])
 
         identity = keep.tile([P, P], F32)
         make_identity(nc, identity[:])
@@ -109,172 +90,143 @@ def tile_multilayerallreduce_pa_s_kernel(tc, x, w_first, w_second, out):
             .bitcast(F32)
             .rearrange("t (r p u) -> t r u p", r=RANKS, u=2)
         )
-        x_grouped = keep.tile([P, RANKS * TOKENS * PACK], BF16, align_bytes=64)
-        x_grouped_words = x_grouped[:].bitcast(F32).rearrange("p (r c u) -> p r c u", r=RANKS, u=2)
-        x_codes = keep.tile([P, RANKS * TOKENS], U32, align_bytes=64)
-        x_scales = keep.tile([P, RANKS * TOKENS], U8, align_bytes=64)
-        idle_sums = psum.tile([TOKENS, WIDTH], F32, name="idle_sums")
+        x_tiles = (
+            keep.tile([P, RANKS * TOKENS * PACK], BF16, align_bytes=64, name="x_grouped"),
+            keep.tile([P, RANKS * TOKENS], U32, align_bytes=64, name="x_codes"),
+            keep.tile([P, RANKS * TOKENS], U8, align_bytes=64, name="x_scales"),
+        )
+        x_grouped_words = x_tiles[0][:].bitcast(F32).rearrange("p (r c u) -> p r c u", r=RANKS, u=2)
 
-        def keep_busy(passes):
-            for e in range(passes):
-                nc.tensor.matmul_mx(
-                    out=idle_sums[:],
-                    lhsT=codes[0][:, :P].bitcast(FP8X4),
-                    lhsT_scale=scales[0][:, :P],
-                    rhs=codes[0][:, :WIDTH].bitcast(FP8X4),
-                    rhs_scale=scales[0][:, :WIDTH],
-                    start=True,
-                    stop=True,
-                )
+        for r in range(RANKS):
+            x_bank = psum.tile([P, 2, TOKENS], F32, name="bank%d" % r)
+            for u in range(2):
+                nc.tensor.transpose(x_bank[:, u, :], x_words[:, r, u, :], identity[:])
+            nc.scalar.copy(out=x_grouped_words[:, r], in_=x_bank[:].rearrange("p u c -> p c u"))
 
-        def x_out(r0, n):
-            bank = psum.tile([P, n, 2, TOKENS], F32, name="x_bank%d" % r0)
-            for r in range(n):
-                for u in range(2):
-                    nc.tensor.transpose(bank[:, r, u, :], x_words[:, r0 + r, u, :], identity[:])
-            nc.scalar.copy(
-                out=x_grouped_words[:, r0 : r0 + n], in_=bank[:].rearrange("p r u c -> p r c u")
+            base = r * WIDTH
+            source = raw_first[r][:].rearrange("p t (c i) -> p c t i", i=RUN)
+            target = first[0][:, base * PACK : (base + WIDTH) * PACK].rearrange(
+                "p (i c t) -> p c t i", i=RUN, t=PACK
             )
-
-        def x_quant(r0, n):
-            nc.vector.quantize_mx(
-                out=x_codes[:, r0 * TOKENS : (r0 + n) * TOKENS].bitcast(FP8X4),
-                scales=x_scales[:, r0 * TOKENS : (r0 + n) * TOKENS],
-                in_=x_grouped[:, r0 * TOKENS * PACK : (r0 + n) * TOKENS * PACK],
-            )
+            middle = RUN // 2
+            nc.scalar.copy(out=target[:, :, :, middle:], in_=source[:, :, :, middle:])
+            if r > 0:
+                quantise(first, base - HALF, HALF)
+            nc.vector.tensor_copy(out=target[:, :, :, :middle], in_=source[:, :, :, :middle])
+            quantise(x_tiles, r * TOKENS, TOKENS)
+            quantise(first, base, HALF)
+        quantise(first, LAST * WIDTH + HALF, HALF)
 
         hidden_sums = psum.tile([P, PACK, TOKENS], F32)
+        filler_sums = psum.tile([P, WIDTH], F32, name="bank7")
+        for i in range(PACK):
+            for r in range(RANKS):
+                if i == 0 and r == 2:
+                    for filler in range(2):
+                        mx_pass(
+                            filler_sums[:], (*first[1:], 0, P), (*first[1:], 0, WIDTH), True, True
+                        )
+                mx_pass(
+                    hidden_sums[:, i, :],
+                    (*first[1:], r * WIDTH + i * P, P),
+                    (*x_tiles[1:], r * TOKENS, TOKENS),
+                    r == 0,
+                    r == LAST,
+                )
 
-        def first_layer_pass(i, r):
-            c0 = r * WIDTH + i * P
-            nc.tensor.matmul_mx(
-                out=hidden_sums[:, i, :],
-                lhsT=codes[0][:, c0 : c0 + P].bitcast(FP8X4),
-                lhsT_scale=scales[0][:, c0 : c0 + P],
-                rhs=x_codes[:, r * TOKENS : (r + 1) * TOKENS].bitcast(FP8X4),
-                rhs_scale=x_scales[:, r * TOKENS : (r + 1) * TOKENS],
-                start=(r == 0),
-                stop=(r == RANKS - 1),
+        def place_of(r, c):
+            for c0, columns in PIECES:
+                if c0 <= c < c0 + columns:
+                    return RANKS * c0 + r * columns + c - c0
+
+        def regroup(engine_copy, r, c0, c1):
+            place = place_of(r, c0)
+            engine_copy(
+                out=second[0][:, place * PACK : (place + c1 - c0) * PACK].rearrange(
+                    "p (c i t) -> p c t i", i=RUN, t=PACK
+                ),
+                in_=raw_second[r][:, :, c0:c1].rearrange("p t (c i) -> p c t i", i=RUN),
             )
 
-        hidden_grouped = keep.tile([P, TOKENS, PACK], BF16, align_bytes=64)
-        hidden_codes = keep.tile([P, TOKENS], U32, align_bytes=64)
-        hidden_scales = keep.tile([P, TOKENS], U8, align_bytes=64)
+        def regroup_quarter(engine_copy, r, quarter):
+            regroup(engine_copy, r, quarter * QUARTER, (quarter + 1) * QUARTER)
 
-        total_sums = []
-        totals = [keep.tile([TOKENS, n], F32, name="total_sb%d" % c0) for c0, n in pieces]
+        def quantise_piece(k, r0, ranks):
+            quantise(second, RANKS * PIECES[k][0] + r0 * PIECES[k][1], ranks * PIECES[k][1])
 
-        def second_layer_pass(r, k, start, stop):
-            c0, n = pieces[k]
-            m0 = place(r, c0)
-            nc.tensor.matmul_mx(
-                out=total_sums[k][:, :n],
-                lhsT=hidden_codes[:].bitcast(FP8X4),
-                lhsT_scale=hidden_scales[:],
-                rhs=codes[1][:, m0 : m0 + n].bitcast(FP8X4),
-                rhs_scale=scales[1][:, m0 : m0 + n],
-                start=start,
-                stop=stop,
-            )
+        vector = nc.vector.tensor_copy
+        scalar = nc.scalar.copy
 
-        def store(k, engine_copy):
-            c0, n = pieces[k]
-            engine_copy(out=totals[k][:], in_=total_sums[k][:, :n])
-            nc.sync.dma_start(
-                out=out[:, :, c0 : c0 + n].rearrange("r t c -> t r c"),
-                in_=totals[k][:].unsqueeze(1).to_broadcast([TOKENS, RANKS, n]),
-            )
+        regroup_quarter(scalar, 0, 2)
+        regroup_quarter(scalar, 0, 3)
+        regroup_quarter(scalar, 1, 2)
+        regroup(vector, 0, 0, HALF)
+        regroup(vector, 1, 0, HALF)
+        quantise_piece(0, 0, 1)
+        quantise_piece(0, 1, 1)
+        regroup(vector, 2, 0, HALF)
 
-        def hidden_copy():
-            nc.scalar.copy(out=hidden_grouped[:], in_=hidden_sums[:].rearrange("p i c -> p c i"))
-
-        def hidden_quant():
-            nc.vector.quantize_mx(
-                out=hidden_codes[:].bitcast(FP8X4),
-                scales=hidden_scales[:],
-                in_=hidden_grouped[:].rearrange("p c i -> p (c i)"),
-            )
-
-        regrouped = {}
-
-        def by_identity(r, quarter, bank, q):
-            if bank not in regrouped:
-                regrouped[bank] = psum.tile([P, 2 * WIDTH], BF16, name=bank)
+        identity_ranks = (1, 2)
+        moved = psum.tile([P, len(identity_ranks) * QUARTER * PACK], BF16, name="bank0")
+        for n, r in enumerate(identity_ranks):
             nc.tensor.matmul(
-                out=regrouped[bank][:, q * WIDTH : (q + 1) * WIDTH],
+                out=moved[:, n * QUARTER * PACK : (n + 1) * QUARTER * PACK],
                 lhsT=identity_bf16[:],
-                rhs=raw[RANKS + r][:, :, quarter * P : (quarter + 1) * P].rearrange("p t c -> p c t"),
+                rhs=raw_second[r][:, :, WIDTH - QUARTER :].rearrange("p t c -> p c t"),
                 start=True,
                 stop=True,
             )
 
-        def identity_copy(r, quarter, bank, q, n):
-            c0 = place(r, quarter * P)
-            nc.scalar.copy(
-                out=grouped[1][:, c0 * PACK : (c0 + n * P) * PACK],
-                in_=regrouped[bank][:, q * WIDTH : (q + n) * WIDTH],
+        hidden_tiles = (
+            keep.tile([P, TOKENS * PACK], BF16, align_bytes=64, name="hidden_grouped"),
+            keep.tile([P, TOKENS], U32, align_bytes=64, name="hidden_codes"),
+            keep.tile([P, TOKENS], U8, align_bytes=64, name="hidden_scales"),
+        )
+        nc.scalar.copy(
+            out=hidden_tiles[0][:].rearrange("p (c i) -> p c i", i=PACK),
+            in_=hidden_sums[:].rearrange("p i c -> p c i"),
+        )
+        quantise(hidden_tiles, 0, TOKENS)
+
+        regroup_quarter(scalar, 2, 2)
+        regroup(vector, LAST, 0, LAST_SHARD_VECTOR_COLUMNS)
+        regroup(scalar, LAST, LAST_SHARD_VECTOR_COLUMNS, HALF)
+        moved_place = place_of(identity_ranks[0], WIDTH - QUARTER)
+        nc.scalar.copy(
+            out=second[0][:, moved_place * PACK : (moved_place + len(identity_ranks) * QUARTER) * PACK],
+            in_=moved[:],
+        )
+        regroup_quarter(scalar, LAST, 3)
+        quantise_piece(0, 2, 1)
+        quantise_piece(0, 3, 1)
+        regroup_quarter(vector, LAST, 2)
+        quantise_piece(1, 0, 2)
+        quantise_piece(1, 2, 2)
+        quantise_piece(2, 0, 2)
+        quantise_piece(2, 2, 1)
+        quantise_piece(2, 3, 1)
+
+        total_sums = [psum.tile([TOKENS, WIDTH], F32, name=name) for name in ("bank5", "bank6", "bank7")]
+        for k, (c0, columns) in enumerate(PIECES):
+            for r in range(RANKS):
+                mx_pass(
+                    total_sums[k][:, :columns],
+                    (*hidden_tiles[1:], 0, TOKENS),
+                    (*second[1:], place_of(r, c0), columns),
+                    r == 0,
+                    r == LAST,
+                )
+
+        def store(c0, columns, total):
+            nc.sync.dma_start(
+                out=out[:, :, c0 : c0 + columns].rearrange("r t c -> t r c"),
+                in_=total[:].unsqueeze(1).to_broadcast([TOKENS, RANKS, columns]),
             )
 
-        for r in range(RANKS):
-            x_out(r, 1)
-            vcopy(first_views(r, 0, 2))
-            scopy(first_views(r, 2, 4))
-            if r > 0:
-                quantise(0, (r - 1) * WIDTH + HALF, HALF)
-            x_quant(r, 1)
-            quantise(0, r * WIDTH, HALF)
-        q = lambda r, i: second_views(r, i * P, (i + 1) * P)
-        scopy(q(0, 2))
-        scopy(q(0, 3))
-        quantise(0, 3 * WIDTH + HALF, HALF)
-        for i in range(PACK):
-            for r in range(RANKS):
-                if i == 0 and r == 2:
-                    keep_busy(2)
-                if i == 0 and r == 3:
-                    keep_busy(0)
-                first_layer_pass(i, r)
-        vcopy(second_views(0, 0, HALF))
-        vcopy(second_views(1, 0, HALF))
-        scopy(q(1, 2))
-        hidden_copy()
-        by_identity(1, 3, "x_bank0", 0)
-        by_identity(2, 3, "x_bank0", 1)
-        total_sums += [
-            psum.tile([TOKENS, WIDTH], F32, name=name) for name in ("total0", "total1", "idle_sums")
-        ]
-        quantise(1, 0, HALF)
-        quantise(1, HALF, HALF)
-        vcopy(second_views(2, 0, HALF))
-        hidden_quant()
-        vcopy(second_views(3, 0, 160))
-        quantise(1, 2 * HALF, HALF)
-        scopy(q(2, 2))
-        scopy(second_views(3, 160, HALF))
-
-        identity_copy(1, 3, "x_bank0", 0, 2)
-        scopy(second_views(3, 384, WIDTH))
-        quantise(1, 3 * HALF, HALF)
-        for r in range(RANKS):
-            second_layer_pass(r, 0, r == 0, r == 3)
-        store(0, nc.scalar.copy)
-
-        vcopy(q(3, 2))
-        quantise(1, 4 * HALF, 2 * P)
-
-        quantise(1, 4 * HALF + 2 * P, 2 * P)
-        for r in range(RANKS):
-            second_layer_pass(r, 1, r == 0, r == 3)
-        quantise(1, 6 * HALF, 2 * P)
-        second_layer_pass(0, 2, True, False)
-        second_layer_pass(1, 2, False, False)
-        last = keep.tile([TOKENS, HALF], F32)
-        nc.scalar.copy(out=last[:, :P], in_=total_sums[1][:, :P])
-        quantise(1, 6 * HALF + 2 * P, 2 * P)
-        second_layer_pass(2, 2, False, False)
-        second_layer_pass(3, 2, False, True)
-        nc.vector.tensor_copy(out=last[:, P:], in_=total_sums[2][:, :P])
-        nc.sync.dma_start(
-            out=out[:, :, HALF:].rearrange("r t c -> t r c"),
-            in_=last[:].unsqueeze(1).to_broadcast([TOKENS, RANKS, HALF]),
-        )
+        total_first = keep.tile([TOKENS, HALF], F32)
+        nc.scalar.copy(out=total_first[:], in_=total_sums[0][:, :HALF])
+        store(0, HALF, total_first)
+        total_last = keep.tile([TOKENS, HALF], F32)
+        nc.scalar.copy(out=total_last[:, :QUARTER], in_=total_sums[1][:, :QUARTER])
+        nc.vector.tensor_copy(out=total_last[:, QUARTER:], in_=total_sums[2][:, :QUARTER])
+        store(HALF, HALF, total_last)

from contextlib import ExitStack

import concourse.mybir as mybir
from concourse.masks import make_identity

BF16 = mybir.dt.bfloat16
F32 = mybir.dt.float32
U32 = mybir.dt.uint32
U8 = mybir.dt.uint8
FP8X4 = mybir.dt.float8_e4m3fn_x4

P = 128
PACK = 4
RUN = 4
RANKS = 4
TOKENS = 128
WIDTH = 512
HALF = WIDTH // 2
QUARTER = WIDTH // 4
LAST = RANKS - 1

PIECES = ((0, HALF), (HALF, QUARTER), (HALF + QUARTER, QUARTER))

LAST_SHARD_VECTOR_COLUMNS = 160

FLOPS = 2 * 2 * RANKS * TOKENS * WIDTH * WIDTH


def tile_multilayerallreduce_pa_s_kernel(tc, x, w_first, w_second, out):
    nc = tc.nc
    with ExitStack() as ctx:
        keep = ctx.enter_context(tc.tile_pool(name="keep", bufs=1))
        psum = ctx.enter_context(tc.psum_pool(name="psum", bufs=1))
        ctx.enter_context(tc.manual_schedule())

        x_rows = keep.tile([TOKENS, RANKS, WIDTH], BF16)
        raw_first = [keep.tile([P, PACK, WIDTH], BF16, name="raw_first%d" % r) for r in range(RANKS)]
        raw_second = [keep.tile([P, PACK, WIDTH], BF16, name="raw_second%d" % r) for r in range(RANKS)]

        def load_columns(raw, weights, c0, c1):
            nc.sync.dma_start(
                out=raw[:, :, c0:c1], in_=weights[:, c0:c1].rearrange("(p t) c -> p t c", t=PACK)
            )

        for r in range(RANKS):
            nc.sync.dma_start(out=x_rows[:, r, :], in_=x[r])
            load_columns(raw_first[r], w_first[r], 0, WIDTH)
        for r in range(LAST):
            load_columns(raw_second[r], w_second[r], 0, WIDTH)
        load_columns(raw_second[LAST], w_second[LAST], 0, HALF)
        load_columns(raw_second[LAST], w_second[LAST], HALF, WIDTH)

        def operand_tiles(layer):
            return (
                keep.tile([P, RANKS * WIDTH * PACK], BF16, align_bytes=64, name="grouped_" + layer),
                keep.tile([P, RANKS * WIDTH], U32, align_bytes=64, name="codes_" + layer),
                keep.tile([P, RANKS * WIDTH], U8, align_bytes=64, name="scales_" + layer),
            )

        first = operand_tiles("first")
        second = operand_tiles("second")

        def quantise(tiles, place, columns):
            grouped, codes, scales = tiles
            nc.vector.quantize_mx(
                out=codes[:, place : place + columns].bitcast(FP8X4),
                scales=scales[:, place : place + columns],
                in_=grouped[:, place * PACK : (place + columns) * PACK],
            )

        def mx_pass(acc, stationary, moving, start, stop):
            (lc, ls, l0, ln), (rc, rs, r0, rn) = stationary, moving
            nc.tensor.matmul_mx(
                out=acc,
                lhsT=lc[:, l0 : l0 + ln].bitcast(FP8X4),
                lhsT_scale=ls[:, l0 : l0 + ln],
                rhs=rc[:, r0 : r0 + rn].bitcast(FP8X4),
                rhs_scale=rs[:, r0 : r0 + rn],
                start=start,
                stop=stop,
            )

        identity = keep.tile([P, P], F32)
        make_identity(nc, identity[:])
        identity_bf16 = keep.tile([P, P], BF16)
        make_identity(nc, identity_bf16[:])
        x_words = (
            x_rows[:]
            .rearrange("t r k -> t (r k)")
            .bitcast(F32)
            .rearrange("t (r p u) -> t r u p", r=RANKS, u=2)
        )
        x_tiles = (
            keep.tile([P, RANKS * TOKENS * PACK], BF16, align_bytes=64, name="x_grouped"),
            keep.tile([P, RANKS * TOKENS], U32, align_bytes=64, name="x_codes"),
            keep.tile([P, RANKS * TOKENS], U8, align_bytes=64, name="x_scales"),
        )
        x_grouped_words = x_tiles[0][:].bitcast(F32).rearrange("p (r c u) -> p r c u", r=RANKS, u=2)

        for r in range(RANKS):
            x_bank = psum.tile([P, 2, TOKENS], F32, name="bank%d" % r)
            for u in range(2):
                nc.tensor.transpose(x_bank[:, u, :], x_words[:, r, u, :], identity[:])
            nc.scalar.copy(out=x_grouped_words[:, r], in_=x_bank[:].rearrange("p u c -> p c u"))

            base = r * WIDTH
            source = raw_first[r][:].rearrange("p t (c i) -> p c t i", i=RUN)
            target = first[0][:, base * PACK : (base + WIDTH) * PACK].rearrange(
                "p (i c t) -> p c t i", i=RUN, t=PACK
            )
            middle = RUN // 2
            nc.scalar.copy(out=target[:, :, :, middle:], in_=source[:, :, :, middle:])
            if r > 0:
                quantise(first, base - HALF, HALF)
            nc.vector.tensor_copy(out=target[:, :, :, :middle], in_=source[:, :, :, :middle])
            quantise(x_tiles, r * TOKENS, TOKENS)
            quantise(first, base, HALF)
        quantise(first, LAST * WIDTH + HALF, HALF)

        hidden_sums = psum.tile([P, PACK, TOKENS], F32)
        filler_sums = psum.tile([P, WIDTH], F32, name="bank7")
        for i in range(PACK):
            for r in range(RANKS):
                if i == 0 and r == 2:
                    for filler in range(2):
                        mx_pass(
                            filler_sums[:], (*first[1:], 0, P), (*first[1:], 0, WIDTH), True, True
                        )
                mx_pass(
                    hidden_sums[:, i, :],
                    (*first[1:], r * WIDTH + i * P, P),
                    (*x_tiles[1:], r * TOKENS, TOKENS),
                    r == 0,
                    r == LAST,
                )

        def place_of(r, c):
            for c0, columns in PIECES:
                if c0 <= c < c0 + columns:
                    return RANKS * c0 + r * columns + c - c0

        def regroup(engine_copy, r, c0, c1):
            place = place_of(r, c0)
            engine_copy(
                out=second[0][:, place * PACK : (place + c1 - c0) * PACK].rearrange(
                    "p (c i t) -> p c t i", i=RUN, t=PACK
                ),
                in_=raw_second[r][:, :, c0:c1].rearrange("p t (c i) -> p c t i", i=RUN),
            )

        def regroup_quarter(engine_copy, r, quarter):
            regroup(engine_copy, r, quarter * QUARTER, (quarter + 1) * QUARTER)

        def quantise_piece(k, r0, ranks):
            quantise(second, RANKS * PIECES[k][0] + r0 * PIECES[k][1], ranks * PIECES[k][1])

        vector = nc.vector.tensor_copy
        scalar = nc.scalar.copy

        regroup_quarter(scalar, 0, 2)
        regroup_quarter(scalar, 0, 3)
        regroup_quarter(scalar, 1, 2)
        regroup(vector, 0, 0, HALF)
        regroup(vector, 1, 0, HALF)
        quantise_piece(0, 0, 1)
        quantise_piece(0, 1, 1)
        regroup(vector, 2, 0, HALF)

        identity_ranks = (1, 2)
        moved = psum.tile([P, len(identity_ranks) * QUARTER * PACK], BF16, name="bank0")
        for n, r in enumerate(identity_ranks):
            nc.tensor.matmul(
                out=moved[:, n * QUARTER * PACK : (n + 1) * QUARTER * PACK],
                lhsT=identity_bf16[:],
                rhs=raw_second[r][:, :, WIDTH - QUARTER :].rearrange("p t c -> p c t"),
                start=True,
                stop=True,
            )

        hidden_tiles = (
            keep.tile([P, TOKENS * PACK], BF16, align_bytes=64, name="hidden_grouped"),
            keep.tile([P, TOKENS], U32, align_bytes=64, name="hidden_codes"),
            keep.tile([P, TOKENS], U8, align_bytes=64, name="hidden_scales"),
        )
        nc.scalar.copy(
            out=hidden_tiles[0][:].rearrange("p (c i) -> p c i", i=PACK),
            in_=hidden_sums[:].rearrange("p i c -> p c i"),
        )
        quantise(hidden_tiles, 0, TOKENS)

        regroup_quarter(scalar, 2, 2)
        regroup(vector, LAST, 0, LAST_SHARD_VECTOR_COLUMNS)
        regroup(scalar, LAST, LAST_SHARD_VECTOR_COLUMNS, HALF)
        moved_place = place_of(identity_ranks[0], WIDTH - QUARTER)
        nc.scalar.copy(
            out=second[0][:, moved_place * PACK : (moved_place + len(identity_ranks) * QUARTER) * PACK],
            in_=moved[:],
        )
        regroup_quarter(scalar, LAST, 3)
        quantise_piece(0, 2, 1)
        quantise_piece(0, 3, 1)
        regroup_quarter(vector, LAST, 2)
        quantise_piece(1, 0, 2)
        quantise_piece(1, 2, 2)
        quantise_piece(2, 0, 2)
        quantise_piece(2, 2, 1)
        quantise_piece(2, 3, 1)

        total_sums = [psum.tile([TOKENS, WIDTH], F32, name=name) for name in ("bank5", "bank6", "bank7")]
        for k, (c0, columns) in enumerate(PIECES):
            for r in range(RANKS):
                mx_pass(
                    total_sums[k][:, :columns],
                    (*hidden_tiles[1:], 0, TOKENS),
                    (*second[1:], place_of(r, c0), columns),
                    r == 0,
                    r == LAST,
                )

        def store(c0, columns, total):
            nc.sync.dma_start(
                out=out[:, :, c0 : c0 + columns].rearrange("r t c -> t r c"),
                in_=total[:].unsqueeze(1).to_broadcast([TOKENS, RANKS, columns]),
            )

        total_first = keep.tile([TOKENS, HALF], F32)
        nc.scalar.copy(out=total_first[:], in_=total_sums[0][:, :HALF])
        store(0, HALF, total_first)
        total_last = keep.tile([TOKENS, HALF], F32)
        nc.scalar.copy(out=total_last[:, :QUARTER], in_=total_sums[1][:, :QUARTER])
        nc.vector.tensor_copy(out=total_last[:, QUARTER:], in_=total_sums[2][:, :QUARTER])
        store(HALF, HALF, total_last)
